import numpy as np
import ml_dtypes


def mxq(x, axis, fmt="e4m3"):
    dtype, down = {"e4m3": (ml_dtypes.float8_e4m3fn, 7), "e5m2": (ml_dtypes.float8_e5m2, 14)}[fmt]
    v = np.moveaxis(np.asarray(x, np.float32).astype(ml_dtypes.bfloat16).astype(np.float64), axis, -1)
    blocks = v.reshape(v.shape[:-1] + (-1, 32))
    amax = np.abs(blocks).max(-1, keepdims=True)
    byte = np.maximum(np.where(amax > 0, np.frexp(amax)[1] - 1 + 127, 0) - down, 1)
    scale = np.exp2(byte - 127.0)
    codes = (blocks / scale).astype(np.float32).astype(dtype).astype(np.float64)
    return np.moveaxis((codes * scale).reshape(v.shape), -1, axis)


WIDE = False


def mx_kscale(k):
    if not WIDE:
        return np.ones(k)
    levels = np.array([10, -10, 5, -5, 0])
    a = np.random.permutation(np.resize(levels, k // 512 * 4)).reshape(k // 512, 4)
    idx = np.arange(k)
    return np.exp2(a[idx // 512, idx % 128 // 32])


BF16 = ml_dtypes.bfloat16


def bf(x):
    return np.asarray(x, np.float32).astype(BF16)


def f64(x):
    return np.asarray(x).astype(np.float64)


B, N, P, C, HID, NB, E, MAXLEN = 2, 8, 3, 256, 128, 63, 1024, 2056
EPS = 1e-5


def setup_inputs():
    s, t = mx_kscale(E), mx_kscale(E)
    return {"h1": bf(np.maximum(np.random.standard_normal((B, N, N, E)), 0.0) * s),
            "edge_mask": bf(np.random.random((B, N, N)) > 0.15),
            "W2": bf(np.random.standard_normal((E, E)) * 1.4 / np.sqrt(E) / s[:, None] * t),
            "b2": bf(np.random.standard_normal(E) * 0.3 * t),
            "W3": bf(np.random.standard_normal((E, E)) * 1.4 / np.sqrt(E) / t[:, None]),
            "b3": bf(np.random.standard_normal(E) * 0.3),
            "ln_g": bf(1.0 + 0.2 * np.random.standard_normal(E)),
            "ln_b": bf(0.2 * np.random.standard_normal(E))}


def reference(h1, edge_mask, W2, b2, W3, b3, ln_g, ln_b):
    h = np.maximum((mxq(f64(h1), 3, "e4m3") @ mxq(f64(W2), 0, "e4m3")) + f64(b2), 0.0)
    h = (mxq(h, 3, "e4m3") @ mxq(f64(W3), 0, "e4m3")) + f64(b3)
    mu = h.mean(-1, keepdims=True)
    var = h.var(-1, keepdims=True)
    h = (h - mu) / np.sqrt(var + EPS) * f64(ln_g) + f64(ln_b)
    return h * f64(edge_mask)[..., None]

@@ -1,0 +1,261 @@
+import concourse.mybir as mybir
+from concourse.masks import make_identity
+
+F32 = mybir.dt.float32
+BF16 = mybir.dt.bfloat16
+U32 = mybir.dt.uint32
+U8 = mybir.dt.uint8
+FP8X4 = mybir.dt.float8_e4m3fn_x4
+ALU = mybir.AluOpType
+ACT = mybir.ActivationFunctionType
+
+P = 128
+E = 1024
+PACK = 4
+K_PASS = P * PACK
+PASSES = E // K_PASS
+BANK = 512
+HALVES = E // BANK
+BLOCKS = BANK // P
+RUN = 4
+VECTOR_COLS = 256
+EPS = 1e-5
+
+FLOPS = 2 * 2 * P * E * E
+
+ROW_B2 = 0
+ROW_B3 = 8
+ROW_G = 16
+ROW_MASK = 24
+ROWS_USED = 32
+
+
+def tile_edgefeaturenet_pb_s_kernel(tc, h1, edge_mask, W2, b2, W3, b3, ln_g, ln_b, out):
+    nc = tc.nc
+    h1_rows = h1.flatten_outer_dims()
+    out_rows = out.flatten_outer_dims()
+    mask_row = edge_mask.rearrange("(o b) i j -> o (b i j)", o=1)
+
+    with (
+        tc.tile_pool(name="keep", bufs=1) as keep,
+        tc.tile_pool(name="stage", bufs=3) as stage,
+        tc.psum_pool(name="psum", bufs=1) as psum,
+    ):
+        w2_raw = keep.tile([P, PASSES, PACK, E], BF16)
+        w3_raw = keep.tile([P, PASSES, PACK, E], BF16)
+        h1_sb = keep.tile([P, E], BF16)
+        w2_view = W2.rearrange("(g p t) n -> p g t n", p=P, t=PACK)
+        w3_view = W3.rearrange("(g t p) n -> p g t n", p=P, t=PACK)
+        for j in range(HALVES):
+            cols = slice(j * BANK, (j + 1) * BANK)
+            nc.sync.dma_start(out=w2_raw[:, 0, :, cols], in_=w2_view[:, 0, :, cols])
+        nc.sync.dma_start(out=h1_sb[:], in_=h1_rows)
+        nc.sync.dma_start(out=w2_raw[:, 1], in_=w2_view[:, 1])
+        for g in range(PASSES):
+            nc.sync.dma_start(out=w3_raw[:, g], in_=w3_view[:, g])
+
+        vecs = keep.tile([P, P], BF16)
+        mask_k0 = keep.tile([P, P], BF16)
+        lnb_k0 = keep.tile([P, E], BF16)
+        nc.vector.memset(vecs[:], 0.0)
+        nc.vector.memset(mask_k0[:], 0.0)
+        nc.vector.memset(lnb_k0[:], 0.0)
+        nc.scalar.dma_start(out=vecs[ROW_B2 : ROW_B2 + 8, :], in_=b2.rearrange("(c p) -> c p", p=P))
+        nc.scalar.dma_start(out=vecs[ROW_B3 : ROW_B3 + 8, :], in_=b3.rearrange("(c p) -> c p", p=P))
+        nc.scalar.dma_start(out=vecs[ROW_G : ROW_G + 8, :], in_=ln_g.rearrange("(c p) -> c p", p=P))
+        nc.scalar.dma_start(out=vecs[ROW_MASK : ROW_MASK + 1, :], in_=mask_row)
+        nc.scalar.dma_start(out=mask_k0[0:1, :], in_=mask_row)
+        nc.scalar.dma_start(out=lnb_k0[0:1, :], in_=ln_b.rearrange("(o e) -> o e", o=1))
+
+        ident_f32 = keep.tile([P, P], F32)
+        ident_bf16 = keep.tile([P, P], BF16)
+        make_identity(nc, ident_f32[:])
+        make_identity(nc, ident_bf16[:])
+        eps = keep.tile([P, 1], F32)
+        nc.vector.memset(eps[:], EPS)
+        table_warm = keep.tile([P, 1], F32)
+        nc.scalar.activation(out=table_warm[:], in_=eps[:], func=ACT.Abs_reciprocal_sqrt)
+
+        vecs_ps = psum.tile([P, P], BF16, tag="vecs_then_y0")
+        nc.tensor.transpose(vecs_ps[:], vecs[:], ident_bf16[:])
+        vecs_t = keep.tile([P, ROWS_USED], BF16)
+        nc.vector.tensor_copy(out=vecs_t[:], in_=vecs_ps[:, :ROWS_USED])
+        mask_col = keep.tile([P, 1], F32)
+        nc.vector.tensor_copy(out=mask_col[:], in_=vecs_ps[:, ROW_MASK : ROW_MASK + 1])
+
+        h1_words = h1_sb[:].bitcast(F32).rearrange("r (g p u) -> r g u p", g=PASSES, u=2)
+        h1_ps = psum.tile([P, PASSES * 2, P], F32, tag="h1_then_y1")
+        for g in range(PASSES):
+            for u in range(2):
+                nc.tensor.transpose(h1_ps[:, 2 * g + u, :], h1_words[:, g, u, :], ident_f32[:])
+
+        b3_ps = psum.tile([P, E], BF16, tag="b3")
+        g_ps = psum.tile([P, E], BF16, tag="ln_g")
+        for c in range(E // P):
+            cols = slice(c * P, (c + 1) * P)
+            nc.tensor.transpose(
+                b3_ps[:, cols], vecs_t[:, ROW_B3 + c : ROW_B3 + c + 1].to_broadcast([P, P]), ident_bf16[:]
+            )
+        for c in range(E // P):
+            cols = slice(c * P, (c + 1) * P)
+            nc.tensor.transpose(
+                g_ps[:, cols], vecs_t[:, ROW_G + c : ROW_G + c + 1].to_broadcast([P, P]), ident_bf16[:]
+            )
+        shift_ps = []
+        for j in range(HALVES):
+            shift_j = psum.tile([P, BANK], F32, name="shift%d" % j)
+            nc.tensor.matmul(
+                shift_j[:], lhsT=mask_k0[:], rhs=lnb_k0[:, j * BANK : (j + 1) * BANK], start=True, stop=True
+            )
+            shift_ps.append(shift_j)
+
+        b3_all = keep.tile([P, E], BF16)
+        nc.scalar.copy(out=b3_all[:], in_=b3_ps[:])
+
+        h1_grouped = keep.tile([P, PASSES * P * PACK], BF16, align_bytes=64)
+        nc.scalar.copy(
+            out=h1_grouped[:].bitcast(F32).rearrange("p (g r u) -> p g r u", g=PASSES, u=2),
+            in_=h1_ps[:].rearrange("p (g u) r -> p g r u", u=2),
+        )
+        h1_codes = keep.tile([P, PASSES * P], U32, align_bytes=64)
+        h1_scales = keep.tile([P, PASSES * P], U8, align_bytes=64)
+        nc.vector.quantize_mx(out=h1_codes[:].bitcast(FP8X4), scales=h1_scales[:], in_=h1_grouped[:])
+
+        w2_codes = keep.tile([P, PASSES, E], U32, align_bytes=64)
+        w2_scales = keep.tile([P, PASSES, E], U8, align_bytes=64)
+        w3_codes = keep.tile([P, PASSES, E], U32, align_bytes=64)
+        w3_scales = keep.tile([P, PASSES, E], U8, align_bytes=64)
+
+        def regroup(raw, g, j):
+            grouped = stage.tile([P, BANK, PACK], BF16, align_bytes=64, name="grouped")
+            src = raw[:, g, :, j * BANK : (j + 1) * BANK].rearrange("p t (c i) -> p c t i", i=RUN)
+            dst = grouped[:].rearrange("p (c i) t -> p c t i", i=RUN)
+            cut = VECTOR_COLS // RUN
+            nc.vector.tensor_copy(out=dst[:, :cut], in_=src[:, :cut])
+            nc.scalar.copy(out=dst[:, cut:], in_=src[:, cut:])
+            return grouped
+
+        def quantise(grouped, codes, scales, g, j):
+            cols = slice(j * BANK, (j + 1) * BANK)
+            nc.vector.quantize_mx(
+                out=codes[:, g, cols].bitcast(FP8X4),
+                scales=scales[:, g, cols],
+                in_=grouped[:].rearrange("p w t -> p (w t)"),
+            )
+
+        hidden_ps = [psum.tile([P, BLOCKS, P], F32, name="hidden%d" % j) for j in range(HALVES)]
+        h_codes = keep.tile([P, PASSES * P], U32, align_bytes=64)
+        h_scales = keep.tile([P, PASSES * P], U8, align_bytes=64)
+
+        def layer1(j):
+            for t in range(BLOCKS):
+                units = slice(j * BANK + t * P, j * BANK + (t + 1) * P)
+                for g in range(PASSES):
+                    tokens = slice(g * P, (g + 1) * P)
+                    nc.tensor.matmul_mx(
+                        out=hidden_ps[j][:, t, :],
+                        lhsT=w2_codes[:, g, units].bitcast(FP8X4),
+                        lhsT_scale=w2_scales[:, g, units],
+                        rhs=h1_codes[:, tokens].bitcast(FP8X4),
+                        rhs_scale=h1_scales[:, tokens],
+                        start=(g == 0),
+                        stop=(g == PASSES - 1),
+                    )
+
+        def hidden_to_mx(j):
+            bias = vecs_t[:, ROW_B2 + j * BLOCKS : ROW_B2 + (j + 1) * BLOCKS]
+            biased = stage.tile([P, P, PACK], BF16, name="biased")
+            nc.vector.tensor_tensor(
+                out=biased[:],
+                in0=hidden_ps[j][:].rearrange("p t r -> p r t"),
+                in1=bias.unsqueeze(1).to_broadcast([P, P, PACK]),
+                op=ALU.add,
+            )
+            h_grouped = stage.tile([P, P * PACK], BF16, align_bytes=64, name="h_grouped")
+            nc.vector.tensor_scalar_max(
+                out=h_grouped[:], in0=biased[:].rearrange("p r t -> p (r t)"), scalar1=0.0
+            )
+            tokens = slice(j * P, (j + 1) * P)
+            nc.vector.quantize_mx(
+                out=h_codes[:, tokens].bitcast(FP8X4), scales=h_scales[:, tokens], in_=h_grouped[:]
+            )
+
+        y_ps = [
+            psum.tile([P, BANK], F32, name="y0", tag="vecs_then_y0"),
+            psum.tile([P, BANK], F32, name="y1", tag="h1_then_y1"),
+        ]
+
+        def layer2(g, j):
+            tokens = slice(g * P, (g + 1) * P)
+            cols = slice(j * BANK, (j + 1) * BANK)
+            nc.tensor.matmul_mx(
+                out=y_ps[j][:],
+                lhsT=h_codes[:, tokens].bitcast(FP8X4),
+                lhsT_scale=h_scales[:, tokens],
+                rhs=w3_codes[:, g, cols].bitcast(FP8X4),
+                rhs_scale=w3_scales[:, g, cols],
+                start=(g == 0),
+                stop=(g == PASSES - 1),
+            )
+
+        pieces = [(g, j) for g in range(PASSES) for j in range(HALVES)]
+        w2_grouped = {}
+        w3_grouped = {}
+        for step, (g, j) in enumerate(pieces):
+            w2_grouped[(g, j)] = regroup(w2_raw, g, j)
+            if step > 0:
+                before = pieces[step - 1]
+                quantise(w2_grouped[before], w2_codes, w2_scales, before[0], before[1])
+        layer1(0)
+        for step, (g, j) in enumerate(pieces):
+            w3_grouped[(g, j)] = regroup(w3_raw, g, j)
+            if step == 0:
+                last = pieces[-1]
+                quantise(w2_grouped[last], w2_codes, w2_scales, last[0], last[1])
+                layer1(1)
+                hidden_to_mx(0)
+            else:
+                before = pieces[step - 1]
+                quantise(w3_grouped[before], w3_codes, w3_scales, before[0], before[1])
+                layer2(before[0], before[1])
+            if step == 1:
+                hidden_to_mx(1)
+        last = pieces[-1]
+        quantise(w3_grouped[last], w3_codes, w3_scales, last[0], last[1])
+        layer2(last[0], last[1])
+
+        z = keep.tile([P, E], F32)
+        stats = keep.tile([P, HALVES, 6], F32)
+        for j in range(HALVES):
+            cols = slice(j * BANK, (j + 1) * BANK)
+            nc.vector.tensor_tensor(out=z[:, cols], in0=y_ps[j][:], in1=b3_all[:, cols], op=ALU.add)
+            nc.vector.bn_stats(out=stats[:, j, :], in_=z[:, cols])
+        mean_var = keep.tile([P, 2], F32)
+        nc.vector.bn_aggr(out=mean_var[:], in_=stats[:].rearrange("p j s -> p (j s)"))
+        rstd = keep.tile([P, 1], F32)
+        nc.scalar.activation(out=rstd[:], in_=mean_var[:, 1:2], func=ACT.Abs_reciprocal_sqrt, bias=eps[:])
+        rstd_mask = keep.tile([P, 1], F32)
+        nc.scalar.activation(out=rstd_mask[:], in_=rstd[:], func=ACT.Copy, scale=mask_col[:])
+        centred = keep.tile([P, E], F32)
+        for j in range(HALVES):
+            cols = slice(j * BANK, (j + 1) * BANK)
+            nc.vector.scalar_tensor_tensor(
+                out=centred[:, cols],
+                in0=z[:, cols],
+                scalar=mean_var[:, 0:1],
+                in1=g_ps[:, cols],
+                op0=ALU.subtract,
+                op1=ALU.mult,
+            )
+        result = keep.tile([P, E], F32)
+        for j in range(HALVES):
+            cols = slice(j * BANK, (j + 1) * BANK)
+            nc.vector.scalar_tensor_tensor(
+                out=result[:, cols],
+                in0=centred[:, cols],
+                scalar=rstd_mask[:],
+                in1=shift_ps[j][:],
+                op0=ALU.mult,
+                op1=ALU.add,
+            )
+            nc.sync.dma_start(out=out_rows[:, cols], in_=result[:, cols])

@@ -40,20 +40,8 @@ def tile_edgefeaturenet_pb_s_kernel(tc, h1, edge_mask, W2, b2, W3, b3, ln_g, ln_
         tc.tile_pool(name="keep", bufs=1) as keep,
         tc.tile_pool(name="stage", bufs=3) as stage,
         tc.psum_pool(name="psum", bufs=1) as psum,
+        tc.manual_schedule(),
     ):
-        w2_raw = keep.tile([P, PASSES, PACK, E], BF16)
-        w3_raw = keep.tile([P, PASSES, PACK, E], BF16)
-        h1_sb = keep.tile([P, E], BF16)
-        w2_view = W2.rearrange("(g p t) n -> p g t n", p=P, t=PACK)
-        w3_view = W3.rearrange("(g t p) n -> p g t n", p=P, t=PACK)
-        for j in range(HALVES):
-            cols = slice(j * BANK, (j + 1) * BANK)
-            nc.sync.dma_start(out=w2_raw[:, 0, :, cols], in_=w2_view[:, 0, :, cols])
-        nc.sync.dma_start(out=h1_sb[:], in_=h1_rows)
-        nc.sync.dma_start(out=w2_raw[:, 1], in_=w2_view[:, 1])
-        for g in range(PASSES):
-            nc.sync.dma_start(out=w3_raw[:, g], in_=w3_view[:, g])
-
         vecs = keep.tile([P, P], BF16)
         mask_k0 = keep.tile([P, P], BF16)
         lnb_k0 = keep.tile([P, E], BF16)
@@ -67,64 +55,38 @@ def tile_edgefeaturenet_pb_s_kernel(tc, h1, edge_mask, W2, b2, W3, b3, ln_g, ln_
         nc.scalar.dma_start(out=mask_k0[0:1, :], in_=mask_row)
         nc.scalar.dma_start(out=lnb_k0[0:1, :], in_=ln_b.rearrange("(o e) -> o e", o=1))
 
+        w2_raw = keep.tile([P, PASSES, PACK, E], BF16)
+        w3_raw = keep.tile([P, PASSES, PACK, E], BF16)
+        h1_sb = keep.tile([P, E], BF16)
+        w2_view = W2.rearrange("(g p t) n -> p g t n", p=P, t=PACK)
+        w3_view = W3.rearrange("(g t p) n -> p g t n", p=P, t=PACK)
+        pieces = [(g, j) for g in range(PASSES) for j in range(HALVES)]
+        for g, j in pieces:
+            cols = slice(j * BANK, (j + 1) * BANK)
+            if (g, j) == pieces[-1]:
+                nc.sync.dma_start(out=h1_sb[:], in_=h1_rows)
+            nc.sync.dma_start(out=w2_raw[:, g, :, cols], in_=w2_view[:, g, :, cols])
+        for g, j in pieces:
+            cols = slice(j * BANK, (j + 1) * BANK)
+            nc.sync.dma_start(out=w3_raw[:, g, :, cols], in_=w3_view[:, g, :, cols])
+
         ident_f32 = keep.tile([P, P], F32)
         ident_bf16 = keep.tile([P, P], BF16)
-        make_identity(nc, ident_f32[:])
         make_identity(nc, ident_bf16[:])
+        make_identity(nc, ident_f32[:])
         eps = keep.tile([P, 1], F32)
         nc.vector.memset(eps[:], EPS)
         table_warm = keep.tile([P, 1], F32)
         nc.scalar.activation(out=table_warm[:], in_=eps[:], func=ACT.Abs_reciprocal_sqrt)
 
-        vecs_ps = psum.tile([P, P], BF16, tag="vecs_then_y0")
-        nc.tensor.transpose(vecs_ps[:], vecs[:], ident_bf16[:])
-        vecs_t = keep.tile([P, ROWS_USED], BF16)
-        nc.vector.tensor_copy(out=vecs_t[:], in_=vecs_ps[:, :ROWS_USED])
-        mask_col = keep.tile([P, 1], F32)
-        nc.vector.tensor_copy(out=mask_col[:], in_=vecs_ps[:, ROW_MASK : ROW_MASK + 1])
-
-        h1_words = h1_sb[:].bitcast(F32).rearrange("r (g p u) -> r g u p", g=PASSES, u=2)
-        h1_ps = psum.tile([P, PASSES * 2, P], F32, tag="h1_then_y1")
-        for g in range(PASSES):
-            for u in range(2):
-                nc.tensor.transpose(h1_ps[:, 2 * g + u, :], h1_words[:, g, u, :], ident_f32[:])
-
-        b3_ps = psum.tile([P, E], BF16, tag="b3")
-        g_ps = psum.tile([P, E], BF16, tag="ln_g")
-        for c in range(E // P):
-            cols = slice(c * P, (c + 1) * P)
-            nc.tensor.transpose(
-                b3_ps[:, cols], vecs_t[:, ROW_B3 + c : ROW_B3 + c + 1].to_broadcast([P, P]), ident_bf16[:]
-            )
-        for c in range(E // P):
-            cols = slice(c * P, (c + 1) * P)
-            nc.tensor.transpose(
-                g_ps[:, cols], vecs_t[:, ROW_G + c : ROW_G + c + 1].to_broadcast([P, P]), ident_bf16[:]
-            )
-        shift_ps = []
-        for j in range(HALVES):
-            shift_j = psum.tile([P, BANK], F32, name="shift%d" % j)
-            nc.tensor.matmul(
-                shift_j[:], lhsT=mask_k0[:], rhs=lnb_k0[:, j * BANK : (j + 1) * BANK], start=True, stop=True
-            )
-            shift_ps.append(shift_j)
-
-        b3_all = keep.tile([P, E], BF16)
-        nc.scalar.copy(out=b3_all[:], in_=b3_ps[:])
-
-        h1_grouped = keep.tile([P, PASSES * P * PACK], BF16, align_bytes=64)
-        nc.scalar.copy(
-            out=h1_grouped[:].bitcast(F32).rearrange("p (g r u) -> p g r u", g=PASSES, u=2),
-            in_=h1_ps[:].rearrange("p (g u) r -> p g r u", u=2),
-        )
-        h1_codes = keep.tile([P, PASSES * P], U32, align_bytes=64)
-        h1_scales = keep.tile([P, PASSES * P], U8, align_bytes=64)
-        nc.vector.quantize_mx(out=h1_codes[:].bitcast(FP8X4), scales=h1_scales[:], in_=h1_grouped[:])
-
         w2_codes = keep.tile([P, PASSES, E], U32, align_bytes=64)
         w2_scales = keep.tile([P, PASSES, E], U8, align_bytes=64)
         w3_codes = keep.tile([P, PASSES, E], U32, align_bytes=64)
         w3_scales = keep.tile([P, PASSES, E], U8, align_bytes=64)
+        h1_codes = keep.tile([P, PASSES * P], U32, align_bytes=64)
+        h1_scales = keep.tile([P, PASSES * P], U8, align_bytes=64)
+        h_codes = keep.tile([P, PASSES * P], U32, align_bytes=64)
+        h_scales = keep.tile([P, PASSES * P], U8, align_bytes=64)
 
         def regroup(raw, g, j):
             grouped = stage.tile([P, BANK, PACK], BF16, align_bytes=64, name="grouped")
@@ -144,8 +106,6 @@ def tile_edgefeaturenet_pb_s_kernel(tc, h1, edge_mask, W2, b2, W3, b3, ln_g, ln_
             )
 
         hidden_ps = [psum.tile([P, BLOCKS, P], F32, name="hidden%d" % j) for j in range(HALVES)]
-        h_codes = keep.tile([P, PASSES * P], U32, align_bytes=64)
-        h_scales = keep.tile([P, PASSES * P], U8, align_bytes=64)
 
         def layer1(j):
             for t in range(BLOCKS):
@@ -162,23 +122,72 @@ def tile_edgefeaturenet_pb_s_kernel(tc, h1, edge_mask, W2, b2, W3, b3, ln_g, ln_
                         stop=(g == PASSES - 1),
                     )
 
-        def hidden_to_mx(j):
+        w2_grouped = []
+        for step, (g, j) in enumerate(pieces):
+            w2_grouped.append(regroup(w2_raw, g, j))
+            if step > 0:
+                quantise(w2_grouped[step - 1], w2_codes, w2_scales, *pieces[step - 1])
+
+        vecs_ps = psum.tile([P, P], BF16, tag="vecs_then_y0")
+        nc.tensor.transpose(vecs_ps[:], vecs[:], ident_bf16[:])
+        vecs_t = keep.tile([P, ROWS_USED], BF16)
+        nc.vector.tensor_copy(out=vecs_t[:], in_=vecs_ps[:, :ROWS_USED])
+        mask_col = keep.tile([P, 1], F32)
+        nc.vector.tensor_copy(out=mask_col[:], in_=vecs_ps[:, ROW_MASK : ROW_MASK + 1])
+
+        h1_words = h1_sb[:].bitcast(F32).rearrange("r (g p u) -> r g u p", g=PASSES, u=2)
+        h1_ps = psum.tile([P, PASSES * 2, P], F32, tag="h1_then_y1")
+        for g in range(PASSES):
+            for u in range(2):
+                nc.tensor.transpose(h1_ps[:, 2 * g + u, :], h1_words[:, g, u, :], ident_f32[:])
+        h1_grouped = keep.tile([P, PASSES * P * PACK], BF16, align_bytes=64)
+        nc.scalar.copy(
+            out=h1_grouped[:].bitcast(F32).rearrange("p (g r u) -> p g r u", g=PASSES, u=2),
+            in_=h1_ps[:].rearrange("p (g u) r -> p g r u", u=2),
+        )
+
+        w3_grouped = [regroup(w3_raw, *pieces[0])]
+        nc.vector.quantize_mx(out=h1_codes[:].bitcast(FP8X4), scales=h1_scales[:], in_=h1_grouped[:])
+        layer1(0)
+        quantise(w2_grouped[-1], w2_codes, w2_scales, *pieces[-1])
+        layer1(1)
+
+        b3_ps = psum.tile([P, E], BF16, tag="b3")
+        g_ps = psum.tile([P, E], BF16, tag="ln_g")
+        for spread, row in ((b3_ps, ROW_B3), (g_ps, ROW_G)):
+            for c in range(E // P):
+                nc.tensor.transpose(
+                    spread[:, c * P : (c + 1) * P],
+                    vecs_t[:, row + c : row + c + 1].to_broadcast([P, P]),
+                    ident_bf16[:],
+                )
+        shift_ps = []
+        for j in range(HALVES):
+            shift_j = psum.tile([P, BANK], F32, name="shift%d" % j)
+            nc.tensor.matmul(
+                shift_j[:], lhsT=mask_k0[:], rhs=lnb_k0[:, j * BANK : (j + 1) * BANK], start=True, stop=True
+            )
+            shift_ps.append(shift_j)
+
+        w3_grouped.append(regroup(w3_raw, *pieces[1]))
+        quantise(w3_grouped[0], w3_codes, w3_scales, *pieces[0])
+        biased = keep.tile([P, HALVES, P, PACK], BF16)
+        for j in range(HALVES):
             bias = vecs_t[:, ROW_B2 + j * BLOCKS : ROW_B2 + (j + 1) * BLOCKS]
-            biased = stage.tile([P, P, PACK], BF16, name="biased")
             nc.vector.tensor_tensor(
-                out=biased[:],
+                out=biased[:, j],
                 in0=hidden_ps[j][:].rearrange("p t r -> p r t"),
                 in1=bias.unsqueeze(1).to_broadcast([P, P, PACK]),
                 op=ALU.add,
             )
-            h_grouped = stage.tile([P, P * PACK], BF16, align_bytes=64, name="h_grouped")
-            nc.vector.tensor_scalar_max(
-                out=h_grouped[:], in0=biased[:].rearrange("p r t -> p (r t)"), scalar1=0.0
-            )
-            tokens = slice(j * P, (j + 1) * P)
-            nc.vector.quantize_mx(
-                out=h_codes[:, tokens].bitcast(FP8X4), scales=h_scales[:, tokens], in_=h_grouped[:]
-            )
+
+        w3_grouped.append(regroup(w3_raw, *pieces[2]))
+        h_grouped = keep.tile([P, PASSES * P * PACK], BF16, align_bytes=64)
+        nc.vector.tensor_scalar_max(
+            out=h_grouped[:], in0=biased[:].rearrange("p j r t -> p (j r t)"), scalar1=0.0
+        )
+        quantise(w3_grouped[1], w3_codes, w3_scales, *pieces[1])
+        nc.vector.quantize_mx(out=h_codes[:].bitcast(FP8X4), scales=h_scales[:], in_=h_grouped[:])
 
         y_ps = [
             psum.tile([P, BANK], F32, name="y0", tag="vecs_then_y0"),
@@ -198,31 +207,16 @@ def tile_edgefeaturenet_pb_s_kernel(tc, h1, edge_mask, W2, b2, W3, b3, ln_g, ln_
                 stop=(g == PASSES - 1),
             )
 
-        pieces = [(g, j) for g in range(PASSES) for j in range(HALVES)]
-        w2_grouped = {}
-        w3_grouped = {}
-        for step, (g, j) in enumerate(pieces):
-            w2_grouped[(g, j)] = regroup(w2_raw, g, j)
-            if step > 0:
-                before = pieces[step - 1]
-                quantise(w2_grouped[before], w2_codes, w2_scales, before[0], before[1])
-        layer1(0)
-        for step, (g, j) in enumerate(pieces):
-            w3_grouped[(g, j)] = regroup(w3_raw, g, j)
-            if step == 0:
-                last = pieces[-1]
-                quantise(w2_grouped[last], w2_codes, w2_scales, last[0], last[1])
-                layer1(1)
-                hidden_to_mx(0)
-            else:
-                before = pieces[step - 1]
-                quantise(w3_grouped[before], w3_codes, w3_scales, before[0], before[1])
-                layer2(before[0], before[1])
-            if step == 1:
-                hidden_to_mx(1)
-        last = pieces[-1]
-        quantise(w3_grouped[last], w3_codes, w3_scales, last[0], last[1])
-        layer2(last[0], last[1])
+        layer2(*pieces[0])
+        layer2(*pieces[1])
+        w3_grouped.append(regroup(w3_raw, *pieces[3]))
+        quantise(w3_grouped[2], w3_codes, w3_scales, *pieces[2])
+        layer2(*pieces[2])
+        quantise(w3_grouped[3], w3_codes, w3_scales, *pieces[3])
+        layer2(*pieces[3])
+
+        b3_all = keep.tile([P, E], BF16)
+        nc.scalar.copy(out=b3_all[:], in_=b3_ps[:])
 
         z = keep.tile([P, E], F32)
         stats = keep.tile([P, HALVES, 6], F32)

@@ -18,7 +18,8 @@ BANK = 512
 HALVES = E // BANK
 BLOCKS = BANK // P
 RUN = 4
-VECTOR_COLS = 256
+W2_VECTOR_COLS = 288
+W3_VECTOR_COLS = 192
 EPS = 1e-5
 
 FLOPS = 2 * 2 * P * E * E
@@ -61,10 +62,9 @@ def tile_edgefeaturenet_pb_s_kernel(tc, h1, edge_mask, W2, b2, W3, b3, ln_g, ln_
         w2_view = W2.rearrange("(g p t) n -> p g t n", p=P, t=PACK)
         w3_view = W3.rearrange("(g t p) n -> p g t n", p=P, t=PACK)
         pieces = [(g, j) for g in range(PASSES) for j in range(HALVES)]
+        nc.sync.dma_start(out=h1_sb[:], in_=h1_rows)
         for g, j in pieces:
             cols = slice(j * BANK, (j + 1) * BANK)
-            if (g, j) == pieces[-1]:
-                nc.sync.dma_start(out=h1_sb[:], in_=h1_rows)
             nc.sync.dma_start(out=w2_raw[:, g, :, cols], in_=w2_view[:, g, :, cols])
         for g, j in pieces:
             cols = slice(j * BANK, (j + 1) * BANK)
@@ -88,11 +88,11 @@ def tile_edgefeaturenet_pb_s_kernel(tc, h1, edge_mask, W2, b2, W3, b3, ln_g, ln_
         h_codes = keep.tile([P, PASSES * P], U32, align_bytes=64)
         h_scales = keep.tile([P, PASSES * P], U8, align_bytes=64)
 
-        def regroup(raw, g, j):
+        def regroup(raw, g, j, vector_cols):
             grouped = stage.tile([P, BANK, PACK], BF16, align_bytes=64, name="grouped")
             src = raw[:, g, :, j * BANK : (j + 1) * BANK].rearrange("p t (c i) -> p c t i", i=RUN)
             dst = grouped[:].rearrange("p (c i) t -> p c t i", i=RUN)
-            cut = VECTOR_COLS // RUN
+            cut = vector_cols // RUN
             nc.vector.tensor_copy(out=dst[:, :cut], in_=src[:, :cut])
             nc.scalar.copy(out=dst[:, cut:], in_=src[:, cut:])
             return grouped
@@ -122,18 +122,22 @@ def tile_edgefeaturenet_pb_s_kernel(tc, h1, edge_mask, W2, b2, W3, b3, ln_g, ln_
                         stop=(g == PASSES - 1),
                     )
 
-        w2_grouped = []
-        for step, (g, j) in enumerate(pieces):
-            w2_grouped.append(regroup(w2_raw, g, j))
-            if step > 0:
-                quantise(w2_grouped[step - 1], w2_codes, w2_scales, *pieces[step - 1])
-
         vecs_ps = psum.tile([P, P], BF16, tag="vecs_then_y0")
         nc.tensor.transpose(vecs_ps[:], vecs[:], ident_bf16[:])
         vecs_t = keep.tile([P, ROWS_USED], BF16)
         nc.vector.tensor_copy(out=vecs_t[:], in_=vecs_ps[:, :ROWS_USED])
         mask_col = keep.tile([P, 1], F32)
         nc.vector.tensor_copy(out=mask_col[:], in_=vecs_ps[:, ROW_MASK : ROW_MASK + 1])
+
+        def spread(row, name):
+            rows_ps = psum.tile([P, E], BF16, name=name)
+            for c in range(E // P):
+                nc.tensor.transpose(
+                    rows_ps[:, c * P : (c + 1) * P],
+                    vecs_t[:, row + c : row + c + 1].to_broadcast([P, P]),
+                    ident_bf16[:],
+                )
+            return rows_ps
 
         h1_words = h1_sb[:].bitcast(F32).rearrange("r (g p u) -> r g u p", g=PASSES, u=2)
         h1_ps = psum.tile([P, PASSES * 2, P], F32, tag="h1_then_y1")
@@ -146,21 +150,21 @@ def tile_edgefeaturenet_pb_s_kernel(tc, h1, edge_mask, W2, b2, W3, b3, ln_g, ln_
             in_=h1_ps[:].rearrange("p (g u) r -> p g r u", u=2),
         )
 
-        w3_grouped = [regroup(w3_raw, *pieces[0])]
+        w2_grouped = [regroup(w2_raw, *pieces[0], W2_VECTOR_COLS)]
         nc.vector.quantize_mx(out=h1_codes[:].bitcast(FP8X4), scales=h1_scales[:], in_=h1_grouped[:])
+        b3_ps = spread(ROW_B3, "b3_ps")
+        b3_all = keep.tile([P, E], BF16)
+        nc.scalar.copy(out=b3_all[:], in_=b3_ps[:])
+        for step in range(1, len(pieces)):
+            w2_grouped.append(regroup(w2_raw, *pieces[step], W2_VECTOR_COLS))
+            quantise(w2_grouped[step - 1], w2_codes, w2_scales, *pieces[step - 1])
         layer1(0)
+
+        w3_grouped = [regroup(w3_raw, *pieces[0], W3_VECTOR_COLS)]
         quantise(w2_grouped[-1], w2_codes, w2_scales, *pieces[-1])
         layer1(1)
 
-        b3_ps = psum.tile([P, E], BF16, tag="b3")
-        g_ps = psum.tile([P, E], BF16, tag="ln_g")
-        for spread, row in ((b3_ps, ROW_B3), (g_ps, ROW_G)):
-            for c in range(E // P):
-                nc.tensor.transpose(
-                    spread[:, c * P : (c + 1) * P],
-                    vecs_t[:, row + c : row + c + 1].to_broadcast([P, P]),
-                    ident_bf16[:],
-                )
+        g_ps = spread(ROW_G, "g_ps")
         shift_ps = []
         for j in range(HALVES):
             shift_j = psum.tile([P, BANK], F32, name="shift%d" % j)
@@ -169,7 +173,7 @@ def tile_edgefeaturenet_pb_s_kernel(tc, h1, edge_mask, W2, b2, W3, b3, ln_g, ln_
             )
             shift_ps.append(shift_j)
 
-        w3_grouped.append(regroup(w3_raw, *pieces[1]))
+        w3_grouped.append(regroup(w3_raw, *pieces[1], W3_VECTOR_COLS))
         quantise(w3_grouped[0], w3_codes, w3_scales, *pieces[0])
         biased = keep.tile([P, HALVES, P, PACK], BF16)
         for j in range(HALVES):
@@ -181,7 +185,7 @@ def tile_edgefeaturenet_pb_s_kernel(tc, h1, edge_mask, W2, b2, W3, b3, ln_g, ln_
                 op=ALU.add,
             )
 
-        w3_grouped.append(regroup(w3_raw, *pieces[2]))
+        w3_grouped.append(regroup(w3_raw, *pieces[2], W3_VECTOR_COLS))
         h_grouped = keep.tile([P, PASSES * P * PACK], BF16, align_bytes=64)
         nc.vector.tensor_scalar_max(
             out=h_grouped[:], in0=biased[:].rearrange("p j r t -> p (j r t)"), scalar1=0.0
@@ -209,14 +213,11 @@ def tile_edgefeaturenet_pb_s_kernel(tc, h1, edge_mask, W2, b2, W3, b3, ln_g, ln_
 
         layer2(*pieces[0])
         layer2(*pieces[1])
-        w3_grouped.append(regroup(w3_raw, *pieces[3]))
+        w3_grouped.append(regroup(w3_raw, *pieces[3], W3_VECTOR_COLS))
         quantise(w3_grouped[2], w3_codes, w3_scales, *pieces[2])
         layer2(*pieces[2])
         quantise(w3_grouped[3], w3_codes, w3_scales, *pieces[3])
         layer2(*pieces[3])
-
-        b3_all = keep.tile([P, E], BF16)
-        nc.scalar.copy(out=b3_all[:], in_=b3_ps[:])
 
         z = keep.tile([P, E], F32)
         stats = keep.tile([P, HALVES, 6], F32)

@@ -20,6 +20,7 @@ BLOCKS = BANK // P
 RUN = 4
 W2_VECTOR_COLS = 288
 W3_VECTOR_COLS = 192
+STORE_COLS = 256
 EPS = 1e-5
 
 FLOPS = 2 * 2 * P * E * E
@@ -62,10 +63,11 @@ def tile_edgefeaturenet_pb_s_kernel(tc, h1, edge_mask, W2, b2, W3, b3, ln_g, ln_
         w2_view = W2.rearrange("(g p t) n -> p g t n", p=P, t=PACK)
         w3_view = W3.rearrange("(g t p) n -> p g t n", p=P, t=PACK)
         pieces = [(g, j) for g in range(PASSES) for j in range(HALVES)]
-        nc.sync.dma_start(out=h1_sb[:], in_=h1_rows)
         for g, j in pieces:
             cols = slice(j * BANK, (j + 1) * BANK)
             nc.sync.dma_start(out=w2_raw[:, g, :, cols], in_=w2_view[:, g, :, cols])
+            if (g, j) == pieces[0]:
+                nc.sync.dma_start(out=h1_sb[:], in_=h1_rows)
         for g, j in pieces:
             cols = slice(j * BANK, (j + 1) * BANK)
             nc.sync.dma_start(out=w3_raw[:, g, :, cols], in_=w3_view[:, g, :, cols])
@@ -139,6 +141,8 @@ def tile_edgefeaturenet_pb_s_kernel(tc, h1, edge_mask, W2, b2, W3, b3, ln_g, ln_
                 )
             return rows_ps
 
+        w2_grouped = [regroup(w2_raw, *pieces[0], W2_VECTOR_COLS)]
+
         h1_words = h1_sb[:].bitcast(F32).rearrange("r (g p u) -> r g u p", g=PASSES, u=2)
         h1_ps = psum.tile([P, PASSES * 2, P], F32, tag="h1_then_y1")
         for g in range(PASSES):
@@ -150,14 +154,14 @@ def tile_edgefeaturenet_pb_s_kernel(tc, h1, edge_mask, W2, b2, W3, b3, ln_g, ln_
             in_=h1_ps[:].rearrange("p (g u) r -> p g r u", u=2),
         )
 
-        w2_grouped = [regroup(w2_raw, *pieces[0], W2_VECTOR_COLS)]
-        nc.vector.quantize_mx(out=h1_codes[:].bitcast(FP8X4), scales=h1_scales[:], in_=h1_grouped[:])
         b3_ps = spread(ROW_B3, "b3_ps")
         b3_all = keep.tile([P, E], BF16)
         nc.scalar.copy(out=b3_all[:], in_=b3_ps[:])
+
         for step in range(1, len(pieces)):
             w2_grouped.append(regroup(w2_raw, *pieces[step], W2_VECTOR_COLS))
             quantise(w2_grouped[step - 1], w2_codes, w2_scales, *pieces[step - 1])
+        nc.vector.quantize_mx(out=h1_codes[:].bitcast(FP8X4), scales=h1_scales[:], in_=h1_grouped[:])
         layer1(0)
 
         w3_grouped = [regroup(w3_raw, *pieces[0], W3_VECTOR_COLS)]
@@ -244,13 +248,15 @@ def tile_edgefeaturenet_pb_s_kernel(tc, h1, edge_mask, W2, b2, W3, b3, ln_g, ln_
             )
         result = keep.tile([P, E], F32)
         for j in range(HALVES):
-            cols = slice(j * BANK, (j + 1) * BANK)
-            nc.vector.scalar_tensor_tensor(
-                out=result[:, cols],
-                in0=centred[:, cols],
-                scalar=rstd_mask[:],
-                in1=shift_ps[j][:],
-                op0=ALU.mult,
-                op1=ALU.add,
-            )
-            nc.sync.dma_start(out=out_rows[:, cols], in_=result[:, cols])
+            for s in range(BANK // STORE_COLS):
+                in_bank = slice(s * STORE_COLS, (s + 1) * STORE_COLS)
+                cols = slice(j * BANK + s * STORE_COLS, j * BANK + (s + 1) * STORE_COLS)
+                nc.vector.scalar_tensor_tensor(
+                    out=result[:, cols],
+                    in0=centred[:, cols],
+                    scalar=rstd_mask[:],
+                    in1=shift_ps[j][:, in_bank],
+                    op0=ALU.mult,
+                    op1=ALU.add,
+                )
+                nc.sync.dma_start(out=out_rows[:, cols], in_=result[:, cols])

@@ -45,17 +45,13 @@ def tile_edgefeaturenet_pb_s_kernel(tc, h1, edge_mask, W2, b2, W3, b3, ln_g, ln_
         tc.manual_schedule(),
     ):
         vecs = keep.tile([P, P], BF16)
-        mask_k0 = keep.tile([P, P], BF16)
-        lnb_k0 = keep.tile([P, E], BF16)
+        lnb_row = keep.tile([P, E], BF16)
         nc.vector.memset(vecs[:], 0.0)
-        nc.vector.memset(mask_k0[:], 0.0)
-        nc.vector.memset(lnb_k0[:], 0.0)
+        nc.vector.memset(lnb_row[:], 0.0)
         nc.scalar.dma_start(out=vecs[ROW_B2 : ROW_B2 + 8, :], in_=b2.rearrange("(c p) -> c p", p=P))
         nc.scalar.dma_start(out=vecs[ROW_B3 : ROW_B3 + 8, :], in_=b3.rearrange("(c p) -> c p", p=P))
         nc.scalar.dma_start(out=vecs[ROW_G : ROW_G + 8, :], in_=ln_g.rearrange("(c p) -> c p", p=P))
         nc.scalar.dma_start(out=vecs[ROW_MASK : ROW_MASK + 1, :], in_=mask_row)
-        nc.scalar.dma_start(out=mask_k0[0:1, :], in_=mask_row)
-        nc.scalar.dma_start(out=lnb_k0[0:1, :], in_=ln_b.rearrange("(o e) -> o e", o=1))
 
         w2_raw = keep.tile([P, PASSES, PACK, E], BF16)
         w3_raw = keep.tile([P, PASSES, PACK, E], BF16)
@@ -71,6 +67,7 @@ def tile_edgefeaturenet_pb_s_kernel(tc, h1, edge_mask, W2, b2, W3, b3, ln_g, ln_
         for g, j in pieces:
             cols = slice(j * BANK, (j + 1) * BANK)
             nc.sync.dma_start(out=w3_raw[:, g, :, cols], in_=w3_view[:, g, :, cols])
+        nc.sync.dma_start(out=lnb_row[ROW_MASK : ROW_MASK + 1, :], in_=ln_b.rearrange("(o e) -> o e", o=1))
 
         ident_f32 = keep.tile([P, P], F32)
         ident_bf16 = keep.tile([P, P], BF16)
@@ -124,6 +121,8 @@ def tile_edgefeaturenet_pb_s_kernel(tc, h1, edge_mask, W2, b2, W3, b3, ln_g, ln_
                         stop=(g == PASSES - 1),
                     )
 
+        w2_grouped = [regroup(w2_raw, *pieces[0], W2_VECTOR_COLS)]
+
         vecs_ps = psum.tile([P, P], BF16, tag="vecs_then_y0")
         nc.tensor.transpose(vecs_ps[:], vecs[:], ident_bf16[:])
         vecs_t = keep.tile([P, ROWS_USED], BF16)
@@ -141,8 +140,6 @@ def tile_edgefeaturenet_pb_s_kernel(tc, h1, edge_mask, W2, b2, W3, b3, ln_g, ln_
                 )
             return rows_ps
 
-        w2_grouped = [regroup(w2_raw, *pieces[0], W2_VECTOR_COLS)]
-
         h1_words = h1_sb[:].bitcast(F32).rearrange("r (g p u) -> r g u p", g=PASSES, u=2)
         h1_ps = psum.tile([P, PASSES * 2, P], F32, tag="h1_then_y1")
         for g in range(PASSES):
@@ -154,11 +151,14 @@ def tile_edgefeaturenet_pb_s_kernel(tc, h1, edge_mask, W2, b2, W3, b3, ln_g, ln_
             in_=h1_ps[:].rearrange("p (g u) r -> p g r u", u=2),
         )
 
+        w2_grouped.append(regroup(w2_raw, *pieces[1], W2_VECTOR_COLS))
+        quantise(w2_grouped[0], w2_codes, w2_scales, *pieces[0])
+
         b3_ps = spread(ROW_B3, "b3_ps")
         b3_all = keep.tile([P, E], BF16)
         nc.scalar.copy(out=b3_all[:], in_=b3_ps[:])
 
-        for step in range(1, len(pieces)):
+        for step in range(2, len(pieces)):
             w2_grouped.append(regroup(w2_raw, *pieces[step], W2_VECTOR_COLS))
             quantise(w2_grouped[step - 1], w2_codes, w2_scales, *pieces[step - 1])
         nc.vector.quantize_mx(out=h1_codes[:].bitcast(FP8X4), scales=h1_scales[:], in_=h1_grouped[:])
@@ -173,7 +173,7 @@ def tile_edgefeaturenet_pb_s_kernel(tc, h1, edge_mask, W2, b2, W3, b3, ln_g, ln_
         for j in range(HALVES):
             shift_j = psum.tile([P, BANK], F32, name="shift%d" % j)
             nc.tensor.matmul(
-                shift_j[:], lhsT=mask_k0[:], rhs=lnb_k0[:, j * BANK : (j + 1) * BANK], start=True, stop=True
+                shift_j[:], lhsT=vecs[:], rhs=lnb_row[:, j * BANK : (j + 1) * BANK], start=True, stop=True
             )
             shift_ps.append(shift_j)
 

import concourse.mybir as mybir
from concourse.masks import make_identity

F32 = mybir.dt.float32
BF16 = mybir.dt.bfloat16
U32 = mybir.dt.uint32
U8 = mybir.dt.uint8
FP8X4 = mybir.dt.float8_e4m3fn_x4
ALU = mybir.AluOpType
ACT = mybir.ActivationFunctionType

P = 128
E = 1024
PACK = 4
K_PASS = P * PACK
PASSES = E // K_PASS
BANK = 512
HALVES = E // BANK
BLOCKS = BANK // P
RUN = 4
W2_VECTOR_COLS = 288
W3_VECTOR_COLS = 192
STORE_COLS = 256
EPS = 1e-5

FLOPS = 2 * 2 * P * E * E

ROW_B2 = 0
ROW_B3 = 8
ROW_G = 16
ROW_MASK = 24
ROWS_USED = 32


def tile_edgefeaturenet_pb_s_kernel(tc, h1, edge_mask, W2, b2, W3, b3, ln_g, ln_b, out):
    nc = tc.nc
    h1_rows = h1.flatten_outer_dims()
    out_rows = out.flatten_outer_dims()
    mask_row = edge_mask.rearrange("(o b) i j -> o (b i j)", o=1)

    with (
        tc.tile_pool(name="keep", bufs=1) as keep,
        tc.tile_pool(name="stage", bufs=3) as stage,
        tc.psum_pool(name="psum", bufs=1) as psum,
        tc.manual_schedule(),
    ):
        vecs = keep.tile([P, P], BF16)
        lnb_row = keep.tile([P, E], BF16)
        nc.vector.memset(vecs[:], 0.0)
        nc.vector.memset(lnb_row[:], 0.0)
        nc.scalar.dma_start(out=vecs[ROW_B2 : ROW_B2 + 8, :], in_=b2.rearrange("(c p) -> c p", p=P))
        nc.scalar.dma_start(out=vecs[ROW_B3 : ROW_B3 + 8, :], in_=b3.rearrange("(c p) -> c p", p=P))
        nc.scalar.dma_start(out=vecs[ROW_G : ROW_G + 8, :], in_=ln_g.rearrange("(c p) -> c p", p=P))
        nc.scalar.dma_start(out=vecs[ROW_MASK : ROW_MASK + 1, :], in_=mask_row)

        w2_raw = keep.tile([P, PASSES, PACK, E], BF16)
        w3_raw = keep.tile([P, PASSES, PACK, E], BF16)
        h1_sb = keep.tile([P, E], BF16)
        w2_view = W2.rearrange("(g p t) n -> p g t n", p=P, t=PACK)
        w3_view = W3.rearrange("(g t p) n -> p g t n", p=P, t=PACK)
        pieces = [(g, j) for g in range(PASSES) for j in range(HALVES)]
        for g, j in pieces:
            cols = slice(j * BANK, (j + 1) * BANK)
            nc.sync.dma_start(out=w2_raw[:, g, :, cols], in_=w2_view[:, g, :, cols])
            if (g, j) == pieces[0]:
                nc.sync.dma_start(out=h1_sb[:], in_=h1_rows)
        for g, j in pieces:
            cols = slice(j * BANK, (j + 1) * BANK)
            nc.sync.dma_start(out=w3_raw[:, g, :, cols], in_=w3_view[:, g, :, cols])
        nc.sync.dma_start(out=lnb_row[ROW_MASK : ROW_MASK + 1, :], in_=ln_b.rearrange("(o e) -> o e", o=1))

        ident_f32 = keep.tile([P, P], F32)
        ident_bf16 = keep.tile([P, P], BF16)
        make_identity(nc, ident_bf16[:])
        make_identity(nc, ident_f32[:])
        eps = keep.tile([P, 1], F32)
        nc.vector.memset(eps[:], EPS)
        table_warm = keep.tile([P, 1], F32)
        nc.scalar.activation(out=table_warm[:], in_=eps[:], func=ACT.Abs_reciprocal_sqrt)

        w2_codes = keep.tile([P, PASSES, E], U32, align_bytes=64)
        w2_scales = keep.tile([P, PASSES, E], U8, align_bytes=64)
        w3_codes = keep.tile([P, PASSES, E], U32, align_bytes=64)
        w3_scales = keep.tile([P, PASSES, E], U8, align_bytes=64)
        h1_codes = keep.tile([P, PASSES * P], U32, align_bytes=64)
        h1_scales = keep.tile([P, PASSES * P], U8, align_bytes=64)
        h_codes = keep.tile([P, PASSES * P], U32, align_bytes=64)
        h_scales = keep.tile([P, PASSES * P], U8, align_bytes=64)

        def regroup(raw, g, j, vector_cols):
            grouped = stage.tile([P, BANK, PACK], BF16, align_bytes=64, name="grouped")
            src = raw[:, g, :, j * BANK : (j + 1) * BANK].rearrange("p t (c i) -> p c t i", i=RUN)
            dst = grouped[:].rearrange("p (c i) t -> p c t i", i=RUN)
            cut = vector_cols // RUN
            nc.vector.tensor_copy(out=dst[:, :cut], in_=src[:, :cut])
            nc.scalar.copy(out=dst[:, cut:], in_=src[:, cut:])
            return grouped

        def quantise(grouped, codes, scales, g, j):
            cols = slice(j * BANK, (j + 1) * BANK)
            nc.vector.quantize_mx(
                out=codes[:, g, cols].bitcast(FP8X4),
                scales=scales[:, g, cols],
                in_=grouped[:].rearrange("p w t -> p (w t)"),
            )

        hidden_ps = [psum.tile([P, BLOCKS, P], F32, name="hidden%d" % j) for j in range(HALVES)]

        def layer1(j):
            for t in range(BLOCKS):
                units = slice(j * BANK + t * P, j * BANK + (t + 1) * P)
                for g in range(PASSES):
                    tokens = slice(g * P, (g + 1) * P)
                    nc.tensor.matmul_mx(
                        out=hidden_ps[j][:, t, :],
                        lhsT=w2_codes[:, g, units].bitcast(FP8X4),
                        lhsT_scale=w2_scales[:, g, units],
                        rhs=h1_codes[:, tokens].bitcast(FP8X4),
                        rhs_scale=h1_scales[:, tokens],
                        start=(g == 0),
                        stop=(g == PASSES - 1),
                    )

        w2_grouped = [regroup(w2_raw, *pieces[0], W2_VECTOR_COLS)]

        vecs_ps = psum.tile([P, P], BF16, tag="vecs_then_y0")
        nc.tensor.transpose(vecs_ps[:], vecs[:], ident_bf16[:])
        vecs_t = keep.tile([P, ROWS_USED], BF16)
        nc.vector.tensor_copy(out=vecs_t[:], in_=vecs_ps[:, :ROWS_USED])
        mask_col = keep.tile([P, 1], F32)
        nc.vector.tensor_copy(out=mask_col[:], in_=vecs_ps[:, ROW_MASK : ROW_MASK + 1])

        def spread(row, name):
            rows_ps = psum.tile([P, E], BF16, name=name)
            for c in range(E // P):
                nc.tensor.transpose(
                    rows_ps[:, c * P : (c + 1) * P],
                    vecs_t[:, row + c : row + c + 1].to_broadcast([P, P]),
                    ident_bf16[:],
                )
            return rows_ps

        h1_words = h1_sb[:].bitcast(F32).rearrange("r (g p u) -> r g u p", g=PASSES, u=2)
        h1_ps = psum.tile([P, PASSES * 2, P], F32, tag="h1_then_y1")
        for g in range(PASSES):
            for u in range(2):
                nc.tensor.transpose(h1_ps[:, 2 * g + u, :], h1_words[:, g, u, :], ident_f32[:])
        h1_grouped = keep.tile([P, PASSES * P * PACK], BF16, align_bytes=64)
        nc.scalar.copy(
            out=h1_grouped[:].bitcast(F32).rearrange("p (g r u) -> p g r u", g=PASSES, u=2),
            in_=h1_ps[:].rearrange("p (g u) r -> p g r u", u=2),
        )

        w2_grouped.append(regroup(w2_raw, *pieces[1], W2_VECTOR_COLS))
        quantise(w2_grouped[0], w2_codes, w2_scales, *pieces[0])

        b3_ps = spread(ROW_B3, "b3_ps")
        b3_all = keep.tile([P, E], BF16)
        nc.scalar.copy(out=b3_all[:], in_=b3_ps[:])

        for step in range(2, len(pieces)):
            w2_grouped.append(regroup(w2_raw, *pieces[step], W2_VECTOR_COLS))
            quantise(w2_grouped[step - 1], w2_codes, w2_scales, *pieces[step - 1])
        nc.vector.quantize_mx(out=h1_codes[:].bitcast(FP8X4), scales=h1_scales[:], in_=h1_grouped[:])
        layer1(0)

        w3_grouped = [regroup(w3_raw, *pieces[0], W3_VECTOR_COLS)]
        quantise(w2_grouped[-1], w2_codes, w2_scales, *pieces[-1])
        layer1(1)

        g_ps = spread(ROW_G, "g_ps")
        shift_ps = []
        for j in range(HALVES):
            shift_j = psum.tile([P, BANK], F32, name="shift%d" % j)
            nc.tensor.matmul(
                shift_j[:], lhsT=vecs[:], rhs=lnb_row[:, j * BANK : (j + 1) * BANK], start=True, stop=True
            )
            shift_ps.append(shift_j)

        w3_grouped.append(regroup(w3_raw, *pieces[1], W3_VECTOR_COLS))
        quantise(w3_grouped[0], w3_codes, w3_scales, *pieces[0])
        biased = keep.tile([P, HALVES, P, PACK], BF16)
        for j in range(HALVES):
            bias = vecs_t[:, ROW_B2 + j * BLOCKS : ROW_B2 + (j + 1) * BLOCKS]
            nc.vector.tensor_tensor(
                out=biased[:, j],
                in0=hidden_ps[j][:].rearrange("p t r -> p r t"),
                in1=bias.unsqueeze(1).to_broadcast([P, P, PACK]),
                op=ALU.add,
            )

        w3_grouped.append(regroup(w3_raw, *pieces[2], W3_VECTOR_COLS))
        h_grouped = keep.tile([P, PASSES * P * PACK], BF16, align_bytes=64)
        nc.vector.tensor_scalar_max(
            out=h_grouped[:], in0=biased[:].rearrange("p j r t -> p (j r t)"), scalar1=0.0
        )
        quantise(w3_grouped[1], w3_codes, w3_scales, *pieces[1])
        nc.vector.quantize_mx(out=h_codes[:].bitcast(FP8X4), scales=h_scales[:], in_=h_grouped[:])

        y_ps = [
            psum.tile([P, BANK], F32, name="y0", tag="vecs_then_y0"),
            psum.tile([P, BANK], F32, name="y1", tag="h1_then_y1"),
        ]

        def layer2(g, j):
            tokens = slice(g * P, (g + 1) * P)
            cols = slice(j * BANK, (j + 1) * BANK)
            nc.tensor.matmul_mx(
                out=y_ps[j][:],
                lhsT=h_codes[:, tokens].bitcast(FP8X4),
                lhsT_scale=h_scales[:, tokens],
                rhs=w3_codes[:, g, cols].bitcast(FP8X4),
                rhs_scale=w3_scales[:, g, cols],
                start=(g == 0),
                stop=(g == PASSES - 1),
            )

        layer2(*pieces[0])
        layer2(*pieces[1])
        w3_grouped.append(regroup(w3_raw, *pieces[3], W3_VECTOR_COLS))
        quantise(w3_grouped[2], w3_codes, w3_scales, *pieces[2])
        layer2(*pieces[2])
        quantise(w3_grouped[3], w3_codes, w3_scales, *pieces[3])
        layer2(*pieces[3])

        z = keep.tile([P, E], F32)
        stats = keep.tile([P, HALVES, 6], F32)
        for j in range(HALVES):
            cols = slice(j * BANK, (j + 1) * BANK)
            nc.vector.tensor_tensor(out=z[:, cols], in0=y_ps[j][:], in1=b3_all[:, cols], op=ALU.add)
            nc.vector.bn_stats(out=stats[:, j, :], in_=z[:, cols])
        mean_var = keep.tile([P, 2], F32)
        nc.vector.bn_aggr(out=mean_var[:], in_=stats[:].rearrange("p j s -> p (j s)"))
        rstd = keep.tile([P, 1], F32)
        nc.scalar.activation(out=rstd[:], in_=mean_var[:, 1:2], func=ACT.Abs_reciprocal_sqrt, bias=eps[:])
        rstd_mask = keep.tile([P, 1], F32)
        nc.scalar.activation(out=rstd_mask[:], in_=rstd[:], func=ACT.Copy, scale=mask_col[:])
        centred = keep.tile([P, E], F32)
        for j in range(HALVES):
            cols = slice(j * BANK, (j + 1) * BANK)
            nc.vector.scalar_tensor_tensor(
                out=centred[:, cols],
                in0=z[:, cols],
                scalar=mean_var[:, 0:1],
                in1=g_ps[:, cols],
                op0=ALU.subtract,
                op1=ALU.mult,
            )
        result = keep.tile([P, E], F32)
        for j in range(HALVES):
            for s in range(BANK // STORE_COLS):
                in_bank = slice(s * STORE_COLS, (s + 1) * STORE_COLS)
                cols = slice(j * BANK + s * STORE_COLS, j * BANK + (s + 1) * STORE_COLS)
                nc.vector.scalar_tensor_tensor(
                    out=result[:, cols],
                    in0=centred[:, cols],
                    scalar=rstd_mask[:],
                    in1=shift_ps[j][:, in_bank],
                    op0=ALU.mult,
                    op1=ALU.add,
                )
                nc.sync.dma_start(out=out_rows[:, cols], in_=result[:, cols])
